import numpy as np
import ml_dtypes


def mxq(x, axis, fmt="e4m3"):
    dtype, down = {"e4m3": (ml_dtypes.float8_e4m3fn, 7), "e5m2": (ml_dtypes.float8_e5m2, 14)}[fmt]
    v = np.moveaxis(np.asarray(x, np.float32).astype(ml_dtypes.bfloat16).astype(np.float64), axis, -1)
    blocks = v.reshape(v.shape[:-1] + (-1, 32))
    amax = np.abs(blocks).max(-1, keepdims=True)
    byte = np.maximum(np.where(amax > 0, np.frexp(amax)[1] - 1 + 127, 0) - down, 1)
    scale = np.exp2(byte - 127.0)
    codes = (blocks / scale).astype(np.float32).astype(dtype).astype(np.float64)
    return np.moveaxis((codes * scale).reshape(v.shape), -1, axis)


WIDE = False


def mx_kscale(k):
    if not WIDE:
        return np.ones(k)
    levels = np.array([10, -10, 5, -5, 0])
    if k % 512:
        return np.exp2(np.random.permutation(np.resize(levels, k // 32))).repeat(32)
    a = np.empty((k // 512, 16))
    for p in range(k // 512):
        a[p, :8] = np.random.permutation(np.resize(levels, 8))
        for g in range(8):
            far = levels[np.abs(levels - a[p, g]) >= 10]
            a[p, g + 8] = far[np.random.randint(len(far))]
    return np.exp2(a.ravel()).repeat(32)


BF16 = ml_dtypes.bfloat16


def bf(x):
    return np.asarray(x, np.float32).astype(BF16)


def f64(x):
    return np.asarray(x).astype(np.float64)


T, H, I, R = 256, 1024, 3584, 512


def silu(v):
    return v / (1.0 + np.exp(-v))


def setup_inputs():
    s, t = mx_kscale(H), mx_kscale(R)
    return {
        "x": bf(np.random.standard_normal((T, H)) * s),
        "Wmean1": bf(np.random.standard_normal((I, H)) / np.sqrt(H) / s),
        "Wmean3": bf(np.random.standard_normal((I, H)) / np.sqrt(H) / s),
        "du1": bf(np.random.standard_normal((I, R)) * 0.5 / np.sqrt(R) / t),
        "dv1": bf(np.random.standard_normal((R, H)) / np.sqrt(H) / s * t[:, None]),
        "du3": bf(np.random.standard_normal((I, R)) * 0.5 / np.sqrt(R) / t),
        "dv3": bf(np.random.standard_normal((R, H)) / np.sqrt(H) / s * t[:, None]),
    }


def reference(x, Wmean1, Wmean3, du1, dv1, du3, dv3):
    xq = mxq(f64(x), 1, "e4m3")
    p3 = xq @ mxq(f64(dv3), 1, "e4m3").T
    up = (xq @ mxq(f64(Wmean3), 1, "e4m3").T) + (mxq(p3, 1, "e4m3") @ mxq(f64(du3), 1, "e4m3").T)
    p1 = xq @ mxq(f64(dv1), 1, "e4m3").T
    gate = (xq @ mxq(f64(Wmean1), 1, "e4m3").T) + (mxq(p1, 1, "e4m3") @ mxq(f64(du1), 1, "e4m3").T)
    return silu(gate) * up

@@ -1,0 +1,219 @@
+from contextlib import ExitStack
+
+import concourse.mybir as mybir
+from concourse.masks import make_identity
+
+BF16 = mybir.dt.bfloat16
+F32 = mybir.dt.float32
+U32 = mybir.dt.uint32
+U8 = mybir.dt.uint8
+FP8X4 = mybir.dt.float8_e4m3fn_x4
+SILU = mybir.ActivationFunctionType.Silu
+
+T, H, I, R = 256, 1024, 3584, 512
+P = 128
+BANK = 512
+N_BANKS = 8
+CHUNK = 512
+N_CHUNKS = I // CHUNK
+PRELOAD = 3
+
+FLOPS = 2 * T * (2 * H * I + 2 * H * R + 2 * R * I)
+
+
+def tile_merge_mixtralsparsemoeblock_pa_kernel(
+    tc, x, Wmean1, Wmean3, du1, dv1, du3, dv3, out
+):
+    nc = tc.nc
+    with ExitStack() as ctx:
+        const = ctx.enter_context(tc.tile_pool(name="const", bufs=1))
+        raw = ctx.enter_context(tc.tile_pool(name="raw", bufs=2 * PRELOAD + 2))
+        grp = ctx.enter_context(tc.tile_pool(name="grp", bufs=8))
+        cod = ctx.enter_context(tc.tile_pool(name="cod", bufs=14))
+        act = ctx.enter_context(tc.tile_pool(name="act", bufs=4))
+        res = ctx.enter_context(tc.tile_pool(name="res", bufs=2 * N_CHUNKS))
+        psum = ctx.enter_context(tc.psum_pool(name="psum", bufs=1))
+        ctx.enter_context(tc.manual_schedule())
+
+        ident = const.tile([P, P], F32, name="ident")
+        make_identity(nc, ident[:])
+        warm = const.tile([P, 8], F32, name="warm")
+        nc.vector.memset(warm[:], 0.0)
+        nc.scalar.activation(out=warm[:, 4:8], in_=warm[:, 0:4], func=SILU)
+
+        def load_rows(tag, src, rows_each):
+            tile = raw.tile([P, rows_each * src.shape[1]], BF16, tag=tag, name=tag)
+            nc.sync.dma_start(out=tile[:], in_=src.rearrange("(p j) k -> p (j k)", j=rows_each))
+            return tile
+
+        chunks = []
+
+        def load_next_chunk():
+            c = len(chunks)
+            if c < N_CHUNKS:
+                rows = slice(c * CHUNK, (c + 1) * CHUNK)
+                w1 = load_rows("w", Wmean1[rows, :], 4)
+                d1 = load_rows("d", du1[rows, :], 4)
+                w3 = load_rows("w", Wmean3[rows, :], 4)
+                d3 = load_rows("d", du3[rows, :], 4)
+                chunks.append([(w1, d1), (w3, d3)])
+
+        ring = [0]
+
+        def next_bank():
+            k = ring[0] % N_BANKS
+            ring[0] = ring[0] + 1
+            return psum.tile([P, BANK], F32, tag="bank%d" % k, name="bank%d" % k)
+
+        def transpose_bank(tile, n_groups, group0, word0):
+            words = tile[:].bitcast(F32)
+            stride = words.shape[1] // n_groups
+            bank = next_bank()
+            for u in range(2):
+                for a in range(2):
+                    src = (group0 + a) * stride + word0
+                    pos = (2 * u + a) * P
+                    nc.tensor.transpose(bank[:, pos : pos + P], words[:, src + u : src + 2 * P : 2], ident[:])
+            return bank
+
+        def transpose_weight(weight, delta):
+            banks = [transpose_bank(weight, 4, 2 * b, 256 * g) for g in range(2) for b in range(2)]
+            if delta is not None:
+                banks.extend([transpose_bank(delta, 4, 2 * b, 0) for b in range(2)])
+            return banks
+
+        def copy_out(on_vector, dst, src):
+            if on_vector:
+                nc.vector.tensor_copy(out=dst, in_=src)
+            else:
+                nc.scalar.copy(out=dst, in_=src)
+
+        def regroup(banks, helped):
+            grouped = []
+            for i in range(len(banks) // 2):
+                tile = grp.tile([P, 4 * BANK], BF16, tag="g", name="g", align_bytes=64)
+                words = tile[:].bitcast(F32)
+                for b in range(2):
+                    copy_out(
+                        b == 1 and i < helped,
+                        words[:, b * BANK : (b + 1) * BANK].rearrange("q (n u) -> q n u", u=2),
+                        banks[2 * i + b][:].rearrange("q (u n) -> q n u", u=2),
+                    )
+                grouped.append(tile)
+            return grouped
+
+        def quantise(pool, tile, tag):
+            width = tile.shape[1] // 4
+            codes = pool.tile([P, width], U32, tag="c" + tag, name="c" + tag, align_bytes=64)
+            scales = pool.tile([P, width], U8, tag="s" + tag, name="s" + tag, align_bytes=64)
+            nc.vector.quantize_mx(out=codes[:].bitcast(FP8X4), scales=scales[:], in_=tile[:])
+            return (codes, scales)
+
+        def mx(acc, still, still0, moving, moving0, width, start, stop):
+            nc.tensor.matmul_mx(
+                out=acc,
+                lhsT=still[0][:, still0 : still0 + P].bitcast(FP8X4),
+                lhsT_scale=still[1][:, still0 : still0 + P],
+                rhs=moving[0][:, moving0 : moving0 + width].bitcast(FP8X4),
+                rhs_scale=moving[1][:, moving0 : moving0 + width],
+                start=start,
+                stop=stop,
+            )
+
+        def by_row(acc):
+            return acc.rearrange("t (j p) -> t p j", j=4)
+
+        def as_rows(tile):
+            return tile.rearrange("t (p j) -> t p j", j=4)
+
+        out_tiles = out.rearrange("(p m) i -> m p i", m=2)
+
+        quantised = {}
+        rounded = {}
+        silu_of = {}
+
+        def transpose(kind, n):
+            if kind == "x":
+                return [transpose_bank(x_raw, 2, 0, 256 * g) for g in range(2)]
+            if kind == "dv":
+                return transpose_weight(dv_raw[n], None)
+            return transpose_weight(chunks[n // 2][n % 2][0], chunks[n // 2][n % 2][1])
+
+        def copy_share(kind, n):
+            return 1 + n % 2 if kind == "half" else 2
+
+        def quantise_operands(kind, grouped):
+            if kind == "x":
+                return [quantise(const, tile, "x") for tile in grouped]
+            return [quantise(cod, tile, "u") for tile in grouped]
+
+        def multiply(kind, n, operands):
+            if kind == "x":
+                quantised["x"] = operands[0]
+            accs = []
+            for m in range(2):
+                if kind == "dv":
+                    acc = next_bank()
+                    for t in range(4):
+                        for g in range(2):
+                            mx(acc[:, t * P : (t + 1) * P], operands[g], t * P,
+                               quantised["x"], 256 * g + m * P, P, g == 0, g == 1)
+                    accs.append(acc)
+                if kind == "half":
+                    acc = next_bank()
+                    mx(acc[:], quantised["x"], m * P, operands[0], 0, BANK, True, False)
+                    mx(acc[:], quantised["x"], 256 + m * P, operands[1], 0, BANK, False, False)
+                    mx(acc[:], quantised[n % 2], m * P, operands[2], 0, BANK, False, True)
+                    accs.append(acc)
+            return accs
+
+        def finish(kind, n, accs, m):
+            if kind == "dv":
+                if m == 0:
+                    rounded[n] = const.tile([P, 4 * T], BF16, name="pg%d" % n, align_bytes=64)
+                copy_out(
+                    m == 0,
+                    rounded[n][:, m * BANK : (m + 1) * BANK].rearrange("q (n t) -> q n t", t=4),
+                    accs[m][:].rearrange("q (t n) -> q n t", t=4),
+                )
+                if m == 1:
+                    quantised[n] = quantise(const, rounded[n], "p%d" % n)
+            if kind == "half" and n % 2 == 0:
+                gated = act.tile([P, CHUNK], F32, tag="silu", name="silu")
+                nc.scalar.activation(out=as_rows(gated[:]), in_=by_row(accs[m][:]), func=SILU)
+                silu_of[m] = gated
+            if kind == "half" and n % 2 == 1:
+                c = n // 2
+                z = res.tile([P, CHUNK], F32, tag="o", name="o")
+                nc.vector.tensor_tensor(
+                    out=as_rows(z[:]),
+                    in0=by_row(accs[m][:]),
+                    in1=as_rows(silu_of[m][:]),
+                    op=mybir.AluOpType.mult,
+                )
+                nc.sync.dma_start(out=out_tiles[m][:, c * CHUNK : (c + 1) * CHUNK], in_=z[:])
+
+        x_raw = load_rows("d", x, 2)
+        dv_raw = [load_rows("w", dv1, 4), load_rows("w", dv3, 4)]
+        for c in range(PRELOAD):
+            load_next_chunk()
+
+        work = [("x", 0), ("dv", 0), ("dv", 1)]
+        work.extend([("half", h) for h in range(2 * N_CHUNKS)])
+        work.append(("end", 0))
+
+        before = ("start", 0)
+        operands = []
+        for kind, n in work:
+            banks = []
+            if kind != "end":
+                banks = transpose(kind, n)
+            if kind in ("dv", "half") and n % 2 == 1:
+                load_next_chunk()
+            accs = multiply(before[0], before[1], operands)
+            grouped = regroup(banks, copy_share(kind, n))
+            operands = quantise_operands(kind, grouped[0:2])
+            finish(before[0], before[1], accs, 0)
+            operands.extend(quantise_operands(kind, grouped[2:3]))
+            finish(before[0], before[1], accs, 1)
+            before = (kind, n)

@@ -28,10 +28,12 @@ def tile_merge_mixtralsparsemoeblock_pa_kernel(
     with ExitStack() as ctx:
         const = ctx.enter_context(tc.tile_pool(name="const", bufs=1))
         raw = ctx.enter_context(tc.tile_pool(name="raw", bufs=2 * PRELOAD + 2))
-        grp = ctx.enter_context(tc.tile_pool(name="grp", bufs=8))
-        cod = ctx.enter_context(tc.tile_pool(name="cod", bufs=14))
+        grp = ctx.enter_context(tc.tile_pool(name="grp", bufs=6))
+        srt = ctx.enter_context(tc.tile_pool(name="srt", bufs=2))
+        srd = ctx.enter_context(tc.tile_pool(name="srd", bufs=3))
+        cod = ctx.enter_context(tc.tile_pool(name="cod", bufs=12))
         act = ctx.enter_context(tc.tile_pool(name="act", bufs=4))
-        res = ctx.enter_context(tc.tile_pool(name="res", bufs=2 * N_CHUNKS))
+        res = ctx.enter_context(tc.tile_pool(name="res", bufs=8))
         psum = ctx.enter_context(tc.psum_pool(name="psum", bufs=1))
         ctx.enter_context(tc.manual_schedule())
 
@@ -65,7 +67,15 @@ def tile_merge_mixtralsparsemoeblock_pa_kernel(
             ring[0] = ring[0] + 1
             return psum.tile([P, BANK], F32, tag="bank%d" % k, name="bank%d" % k)
 
-        def transpose_bank(tile, n_groups, group0, word0):
+        def sort_words(pool, tag, tile):
+            out_tile = pool.tile([P, tile.shape[1]], BF16, tag=tag, name=tag)
+            nc.vector.tensor_copy(
+                out=out_tile[:].bitcast(F32).rearrange("p (b u w) -> p b u w", u=2, w=P),
+                in_=tile[:].bitcast(F32).rearrange("p (b w u) -> p b u w", u=2, w=P),
+            )
+            return out_tile
+
+        def transpose_bank(tile, n_groups, group0, word0, is_sorted):
             words = tile[:].bitcast(F32)
             stride = words.shape[1] // n_groups
             bank = next_bank()
@@ -73,13 +83,18 @@ def tile_merge_mixtralsparsemoeblock_pa_kernel(
                 for a in range(2):
                     src = (group0 + a) * stride + word0
                     pos = (2 * u + a) * P
-                    nc.tensor.transpose(bank[:, pos : pos + P], words[:, src + u : src + 2 * P : 2], ident[:])
+                    if is_sorted:
+                        in_words = words[:, src + u * P : src + (u + 1) * P]
+                    else:
+                        in_words = words[:, src + u : src + 2 * P : 2]
+                    nc.tensor.transpose(bank[:, pos : pos + P], in_words, ident[:])
             return bank
 
         def transpose_weight(weight, delta):
-            banks = [transpose_bank(weight, 4, 2 * b, 256 * g) for g in range(2) for b in range(2)]
+            is_sorted = delta is not None
+            banks = [transpose_bank(weight, 4, 2 * b, 256 * g, is_sorted) for g in range(2) for b in range(2)]
             if delta is not None:
-                banks.extend([transpose_bank(delta, 4, 2 * b, 0) for b in range(2)])
+                banks.extend([transpose_bank(delta, 4, 2 * b, 0, is_sorted) for b in range(2)])
             return banks
 
         def copy_out(on_vector, dst, src):
@@ -130,17 +145,27 @@ def tile_merge_mixtralsparsemoeblock_pa_kernel(
 
         quantised = {}
         rounded = {}
+        sorted_w = {}
+        sorted_d = {}
         silu_of = {}
 
         def transpose(kind, n):
             if kind == "x":
-                return [transpose_bank(x_raw, 2, 0, 256 * g) for g in range(2)]
+                return [transpose_bank(x_raw, 2, 0, 256 * g, False) for g in range(2)]
             if kind == "dv":
                 return transpose_weight(dv_raw[n], None)
-            return transpose_weight(chunks[n // 2][n % 2][0], chunks[n // 2][n % 2][1])
+            return transpose_weight(sorted_w[n], sorted_d[n])
+
+        def sort_weight(h):
+            if h < 2 * N_CHUNKS:
+                sorted_w[h] = sort_words(srt, "sw", chunks[h // 2][h % 2][0])
+
+        def sort_delta(h):
+            if h < 2 * N_CHUNKS:
+                sorted_d[h] = sort_words(srd, "sd", chunks[h // 2][h % 2][1])
 
         def copy_share(kind, n):
-            return 1 + n % 2 if kind == "half" else 2
+            return 0 if kind == "half" else 2
 
         def quantise_operands(kind, grouped):
             if kind == "x":
@@ -208,12 +233,25 @@ def tile_merge_mixtralsparsemoeblock_pa_kernel(
             banks = []
             if kind != "end":
                 banks = transpose(kind, n)
-            if kind in ("dv", "half") and n % 2 == 1:
+            if kind == "dv" and n == 1:
                 load_next_chunk()
             accs = multiply(before[0], before[1], operands)
             grouped = regroup(banks, copy_share(kind, n))
+            if kind == "half":
+                sort_weight(n + 1)
             operands = quantise_operands(kind, grouped[0:2])
+            if kind == "dv" and n == 1:
+                sort_weight(0)
+                sort_delta(0)
             finish(before[0], before[1], accs, 0)
+            if kind == "dv" and n == 1:
+                sort_delta(1)
+            if kind == "half" and n % 2 == 1:
+                sort_delta(n + 1)
             operands.extend(quantise_operands(kind, grouped[2:3]))
+            if kind == "half" and n % 2 == 1:
+                sort_delta(n + 2)
             finish(before[0], before[1], accs, 1)
+            if kind == "half" and n % 2 == 0:
+                load_next_chunk()
             before = (kind, n)

@@ -67,34 +67,29 @@ def tile_merge_mixtralsparsemoeblock_pa_kernel(
             ring[0] = ring[0] + 1
             return psum.tile([P, BANK], F32, tag="bank%d" % k, name="bank%d" % k)
 
-        def sort_words(pool, tag, tile):
+        def sort_words(pool, tag, tile, run):
             out_tile = pool.tile([P, tile.shape[1]], BF16, tag=tag, name=tag)
             nc.vector.tensor_copy(
-                out=out_tile[:].bitcast(F32).rearrange("p (b u w) -> p b u w", u=2, w=P),
-                in_=tile[:].bitcast(F32).rearrange("p (b w u) -> p b u w", u=2, w=P),
+                out=out_tile[:].bitcast(F32).rearrange("p (b u s j) -> p b u s j", u=2, j=run, s=P // run),
+                in_=tile[:].bitcast(F32).rearrange("p (b s u j) -> p b u s j", u=2, j=run, s=P // run),
             )
             return out_tile
 
-        def transpose_bank(tile, n_groups, group0, word0, is_sorted):
+        def transpose_bank(tile, n_groups, group0, word0):
             words = tile[:].bitcast(F32)
             stride = words.shape[1] // n_groups
             bank = next_bank()
             for u in range(2):
                 for a in range(2):
-                    src = (group0 + a) * stride + word0
+                    src = (group0 + a) * stride + word0 + u * P
                     pos = (2 * u + a) * P
-                    if is_sorted:
-                        in_words = words[:, src + u * P : src + (u + 1) * P]
-                    else:
-                        in_words = words[:, src + u : src + 2 * P : 2]
-                    nc.tensor.transpose(bank[:, pos : pos + P], in_words, ident[:])
+                    nc.tensor.transpose(bank[:, pos : pos + P], words[:, src : src + P], ident[:])
             return bank
 
         def transpose_weight(weight, delta):
-            is_sorted = delta is not None
-            banks = [transpose_bank(weight, 4, 2 * b, 256 * g, is_sorted) for g in range(2) for b in range(2)]
+            banks = [transpose_bank(weight, 4, 2 * b, 256 * g) for g in range(2) for b in range(2)]
             if delta is not None:
-                banks.extend([transpose_bank(delta, 4, 2 * b, 0, is_sorted) for b in range(2)])
+                banks.extend([transpose_bank(delta, 4, 2 * b, 0) for b in range(2)])
             return banks
 
         def copy_out(on_vector, dst, src):
@@ -147,25 +142,27 @@ def tile_merge_mixtralsparsemoeblock_pa_kernel(
         rounded = {}
         sorted_w = {}
         sorted_d = {}
+        sorted_x = {}
+        sorted_dv = {}
         silu_of = {}
 
         def transpose(kind, n):
             if kind == "x":
-                return [transpose_bank(x_raw, 2, 0, 256 * g, False) for g in range(2)]
+                return [transpose_bank(sorted_x[0], 2, 0, 256 * g) for g in range(2)]
             if kind == "dv":
-                return transpose_weight(dv_raw[n], None)
+                return transpose_weight(sorted_dv[n], None)
             return transpose_weight(sorted_w[n], sorted_d[n])
 
         def sort_weight(h):
             if h < 2 * N_CHUNKS:
-                sorted_w[h] = sort_words(srt, "sw", chunks[h // 2][h % 2][0])
+                sorted_w[h] = sort_words(srt, "sw", chunks[h // 2][h % 2][0], 8)
 
         def sort_delta(h):
             if h < 2 * N_CHUNKS:
-                sorted_d[h] = sort_words(srd, "sd", chunks[h // 2][h % 2][1])
+                sorted_d[h] = sort_words(srd, "sd", chunks[h // 2][h % 2][1], 1)
 
         def copy_share(kind, n):
-            return 0 if kind == "half" else 2
+            return 0
 
         def quantise_operands(kind, grouped):
             if kind == "x":
@@ -229,6 +226,8 @@ def tile_merge_mixtralsparsemoeblock_pa_kernel(
 
         before = ("start", 0)
         operands = []
+        sorted_x[0] = sort_words(const, "x_sorted", x_raw, 8)
+        sorted_dv[0] = sort_words(srt, "sw", dv_raw[0], 8)
         for kind, n in work:
             banks = []
             if kind != "end":
@@ -240,7 +239,9 @@ def tile_merge_mixtralsparsemoeblock_pa_kernel(
             if kind == "half":
                 sort_weight(n + 1)
             operands = quantise_operands(kind, grouped[0:2])
-            if kind == "dv" and n == 1:
+            if kind == "x":
+                sorted_dv[1] = sort_words(srt, "sw", dv_raw[1], 8)
+            if kind == "dv" and n == 0:
                 sort_weight(0)
                 sort_delta(0)
             finish(before[0], before[1], accs, 0)

@@ -14,8 +14,10 @@ T, H, I, R = 256, 1024, 3584, 512
 P = 128
 BANK = 512
 N_BANKS = 8
-CHUNK = 512
-N_CHUNKS = I // CHUNK
+WIDTHS = [512] * 7
+STARTS = [sum(WIDTHS[:c]) for c in range(len(WIDTHS))]
+N_CHUNKS = len(WIDTHS)
+N_HALVES = 2 * N_CHUNKS
 PRELOAD = 3
 
 FLOPS = 2 * T * (2 * H * I + 2 * H * R + 2 * R * I)
@@ -27,11 +29,11 @@ def tile_merge_mixtralsparsemoeblock_pa_kernel(
     nc = tc.nc
     with ExitStack() as ctx:
         const = ctx.enter_context(tc.tile_pool(name="const", bufs=1))
-        raw = ctx.enter_context(tc.tile_pool(name="raw", bufs=2 * PRELOAD + 2))
-        grp = ctx.enter_context(tc.tile_pool(name="grp", bufs=6))
-        srt = ctx.enter_context(tc.tile_pool(name="srt", bufs=2))
-        srd = ctx.enter_context(tc.tile_pool(name="srd", bufs=3))
-        cod = ctx.enter_context(tc.tile_pool(name="cod", bufs=12))
+        raw = ctx.enter_context(tc.tile_pool(name="raw", bufs=8))
+        srt = ctx.enter_context(tc.tile_pool(name="srt", bufs=3))
+        srd = ctx.enter_context(tc.tile_pool(name="srd", bufs=5))
+        grp = ctx.enter_context(tc.tile_pool(name="grp", bufs=3))
+        cod = ctx.enter_context(tc.tile_pool(name="cod", bufs=4))
         act = ctx.enter_context(tc.tile_pool(name="act", bufs=4))
         res = ctx.enter_context(tc.tile_pool(name="res", bufs=8))
         psum = ctx.enter_context(tc.psum_pool(name="psum", bufs=1))
@@ -43,22 +45,30 @@ def tile_merge_mixtralsparsemoeblock_pa_kernel(
         nc.vector.memset(warm[:], 0.0)
         nc.scalar.activation(out=warm[:, 4:8], in_=warm[:, 0:4], func=SILU)
 
-        def load_rows(tag, src, rows_each):
+        def load_dv(dv):
+            tile = raw.tile([P, 4 * H], BF16, tag="w", name="w")
+            nc.sync.dma_start(
+                out=tile[:].rearrange("p (h f) -> p h f", h=2),
+                in_=dv.rearrange("(h p e) k -> p h (e k)", h=2, e=2),
+            )
+            return tile
+
+        def load_rows(tag, src):
+            rows_each = src.shape[0] // P
             tile = raw.tile([P, rows_each * src.shape[1]], BF16, tag=tag, name=tag)
             nc.sync.dma_start(out=tile[:], in_=src.rearrange("(p j) k -> p (j k)", j=rows_each))
             return tile
 
-        chunks = []
+        raw_w = {}
+        raw_d = {}
 
-        def load_next_chunk():
-            c = len(chunks)
+        def load_chunk(c):
             if c < N_CHUNKS:
-                rows = slice(c * CHUNK, (c + 1) * CHUNK)
-                w1 = load_rows("w", Wmean1[rows, :], 4)
-                d1 = load_rows("d", du1[rows, :], 4)
-                w3 = load_rows("w", Wmean3[rows, :], 4)
-                d3 = load_rows("d", du3[rows, :], 4)
-                chunks.append([(w1, d1), (w3, d3)])
+                rows = slice(STARTS[c], STARTS[c] + WIDTHS[c])
+                raw_w[2 * c] = load_rows("w", Wmean1[rows, :])
+                raw_d[2 * c] = load_rows("d", du1[rows, :])
+                raw_w[2 * c + 1] = load_rows("w", Wmean3[rows, :])
+                raw_d[2 * c + 1] = load_rows("d", du3[rows, :])
 
         ring = [0]
 
@@ -67,57 +77,69 @@ def tile_merge_mixtralsparsemoeblock_pa_kernel(
             ring[0] = ring[0] + 1
             return psum.tile([P, BANK], F32, tag="bank%d" % k, name="bank%d" % k)
 
-        def sort_words(pool, tag, tile, run):
-            out_tile = pool.tile([P, tile.shape[1]], BF16, tag=tag, name=tag)
-            nc.vector.tensor_copy(
-                out=out_tile[:].bitcast(F32).rearrange("p (b u s j) -> p b u s j", u=2, j=run, s=P // run),
-                in_=tile[:].bitcast(F32).rearrange("p (b s u j) -> p b u s j", u=2, j=run, s=P // run),
-            )
-            return out_tile
-
-        def transpose_bank(tile, n_groups, group0, word0):
-            words = tile[:].bitcast(F32)
-            stride = words.shape[1] // n_groups
-            bank = next_bank()
-            for u in range(2):
-                for a in range(2):
-                    src = (group0 + a) * stride + word0 + u * P
-                    pos = (2 * u + a) * P
-                    nc.tensor.transpose(bank[:, pos : pos + P], words[:, src : src + P], ident[:])
-            return bank
-
-        def transpose_weight(weight, delta):
-            banks = [transpose_bank(weight, 4, 2 * b, 256 * g) for g in range(2) for b in range(2)]
-            if delta is not None:
-                banks.extend([transpose_bank(delta, 4, 2 * b, 0) for b in range(2)])
-            return banks
-
-        def copy_out(on_vector, dst, src):
+        def copy_by(on_vector, dst, src):
             if on_vector:
                 nc.vector.tensor_copy(out=dst, in_=src)
             else:
                 nc.scalar.copy(out=dst, in_=src)
 
-        def regroup(banks, helped):
-            grouped = []
-            for i in range(len(banks) // 2):
-                tile = grp.tile([P, 4 * BANK], BF16, tag="g", name="g", align_bytes=64)
-                words = tile[:].bitcast(F32)
-                for b in range(2):
-                    copy_out(
-                        b == 1 and i < helped,
-                        words[:, b * BANK : (b + 1) * BANK].rearrange("q (n u) -> q n u", u=2),
-                        banks[2 * i + b][:].rearrange("q (u n) -> q n u", u=2),
-                    )
-                grouped.append(tile)
-            return grouped
+        def take_odd(pool, tag, tile):
+            odd = pool.tile([P, tile.shape[1] // 2], BF16, tag=tag, name=tag)
+            nc.vector.tensor_copy(
+                out=odd[:].bitcast(F32).rearrange("p (b i h j) -> p b i h j", i=8, h=2, j=8),
+                in_=tile[:].bitcast(F32).rearrange("p (b h i u j) -> p b i h u j", h=2, i=8, u=2, j=8)[:, :, :, :, 1],
+            )
+            return odd
 
-        def quantise(pool, tile, tag):
-            width = tile.shape[1] // 4
+        def close_up(tile):
+            runs = tile[:].bitcast(F32).rearrange("p (b h i u j) -> p b h i u j", h=2, i=8, u=2, j=8)
+            nc.vector.tensor_copy(out=runs[:, :, 0, :, 1], in_=runs[:, :, 1, :, 0])
+
+        def transpose_bank(pair, row_words, groups, word0):
+            bank = next_bank()
+            for u in range(2):
+                words = pair[u][:].bitcast(F32)
+                for a in range(2):
+                    src = (groups[a] * row_words + word0) // (1 + u)
+                    pos = (2 * u + a) * P
+                    nc.tensor.transpose(bank[:, pos : pos + P], words[:, src : src + P], ident[:])
+            return bank
+
+        def regroup(tag, banks, on_vector):
+            tile = grp.tile([P, 2 * BANK * len(banks)], BF16, tag=tag, name=tag, align_bytes=64)
+            words = tile[:].bitcast(F32)
+            for i in range(len(banks)):
+                copy_by(
+                    i in on_vector,
+                    words[:, i * BANK : (i + 1) * BANK].rearrange("q (n u) -> q n u", u=2),
+                    banks[i][:].rearrange("q (u n) -> q n u", u=2),
+                )
+            return tile
+
+        def regroup_dv(banks, on_vector):
+            tile = grp.tile([P, 2 * BANK * len(banks)], BF16, tag="gw", name="gw", align_bytes=64)
+            places = tile[:].bitcast(F32).rearrange("q (g u e n) -> q g e u n", g=2, u=2, e=2)
+            for n in range(len(banks)):
+                for u in range(2):
+                    copy_by(
+                        n in on_vector,
+                        places[:, n // 2, n % 2, u].rearrange("q (i h j w) -> q i h j w", h=2, j=8, w=2),
+                        banks[n][:].rearrange("q (w h i u j) -> q u i h j w", w=2, h=2, i=8, u=2)[:, u],
+                    )
+            return tile
+
+        def new_codes(pool, width, tag):
             codes = pool.tile([P, width], U32, tag="c" + tag, name="c" + tag, align_bytes=64)
             scales = pool.tile([P, width], U8, tag="s" + tag, name="s" + tag, align_bytes=64)
-            nc.vector.quantize_mx(out=codes[:].bitcast(FP8X4), scales=scales[:], in_=tile[:])
             return (codes, scales)
+
+        def quantise(pair, tile, first, width):
+            columns = slice(first, first + width)
+            nc.vector.quantize_mx(
+                out=pair[0][:, columns].bitcast(FP8X4),
+                scales=pair[1][:, columns],
+                in_=tile[:, 4 * first : 4 * (first + width)],
+            )
 
         def mx(acc, still, still0, moving, moving0, width, start, stop):
             nc.tensor.matmul_mx(
@@ -130,129 +152,172 @@ def tile_merge_mixtralsparsemoeblock_pa_kernel(
                 stop=stop,
             )
 
-        def by_row(acc):
-            return acc.rearrange("t (j p) -> t p j", j=4)
-
-        def as_rows(tile):
-            return tile.rearrange("t (p j) -> t p j", j=4)
-
         out_tiles = out.rearrange("(p m) i -> m p i", m=2)
 
         quantised = {}
         rounded = {}
-        sorted_w = {}
-        sorted_d = {}
-        sorted_x = {}
-        sorted_dv = {}
+        odd_w = {}
+        odd_d = {}
         silu_of = {}
 
-        def transpose(kind, n):
-            if kind == "x":
-                return [transpose_bank(sorted_x[0], 2, 0, 256 * g) for g in range(2)]
-            if kind == "dv":
-                return transpose_weight(sorted_dv[n], None)
-            return transpose_weight(sorted_w[n], sorted_d[n])
+        def width_of(h):
+            return WIDTHS[h // 2]
 
-        def sort_weight(h):
-            if h < 2 * N_CHUNKS:
-                sorted_w[h] = sort_words(srt, "sw", chunks[h // 2][h % 2][0], 8)
+        def take_odd_w(h):
+            if h < N_HALVES:
+                odd_w[h] = take_odd(srt, "ow", raw_w[h])
 
-        def sort_delta(h):
-            if h < 2 * N_CHUNKS:
-                sorted_d[h] = sort_words(srd, "sd", chunks[h // 2][h % 2][1], 1)
+        def take_odd_d(h):
+            if h < N_HALVES:
+                odd_d[h] = take_odd(srd, "od", raw_d[h])
 
-        def copy_share(kind, n):
-            return 0
+        def close_up_w(h):
+            if h < N_HALVES:
+                close_up(raw_w[h])
 
-        def quantise_operands(kind, grouped):
-            if kind == "x":
-                return [quantise(const, tile, "x") for tile in grouped]
-            return [quantise(cod, tile, "u") for tile in grouped]
+        def close_up_d(h):
+            if h < N_HALVES:
+                close_up(raw_d[h])
 
-        def multiply(kind, n, operands):
-            if kind == "x":
-                quantised["x"] = operands[0]
-            accs = []
-            for m in range(2):
-                if kind == "dv":
-                    acc = next_bank()
-                    for t in range(4):
-                        for g in range(2):
-                            mx(acc[:, t * P : (t + 1) * P], operands[g], t * P,
-                               quantised["x"], 256 * g + m * P, P, g == 0, g == 1)
-                    accs.append(acc)
-                if kind == "half":
-                    acc = next_bank()
-                    mx(acc[:], quantised["x"], m * P, operands[0], 0, BANK, True, False)
-                    mx(acc[:], quantised["x"], 256 + m * P, operands[1], 0, BANK, False, False)
-                    mx(acc[:], quantised[n % 2], m * P, operands[2], 0, BANK, False, True)
-                    accs.append(acc)
-            return accs
+        def transpose_half(h):
+            pairs = [(2 * b, 2 * b + 1) for b in range(width_of(h) // 256)]
+            w_banks = [transpose_bank((raw_w[h], odd_w[h]), H // 2, pair, 256 * g) for g in range(2) for pair in pairs]
+            d_banks = [transpose_bank((raw_d[h], odd_d[h]), R // 2, pair, 0) for pair in pairs]
+            return w_banks, d_banks
 
-        def finish(kind, n, accs, m):
-            if kind == "dv":
-                if m == 0:
-                    rounded[n] = const.tile([P, 4 * T], BF16, name="pg%d" % n, align_bytes=64)
-                copy_out(
-                    m == 0,
-                    rounded[n][:, m * BANK : (m + 1) * BANK].rearrange("q (n t) -> q n t", t=4),
-                    accs[m][:].rearrange("q (t n) -> q n t", t=4),
-                )
-                if m == 1:
-                    quantised[n] = quantise(const, rounded[n], "p%d" % n)
-            if kind == "half" and n % 2 == 0:
-                gated = act.tile([P, CHUNK], F32, tag="silu", name="silu")
-                nc.scalar.activation(out=as_rows(gated[:]), in_=by_row(accs[m][:]), func=SILU)
+        def multiply_dv(codes, m):
+            acc = next_bank()
+            for t in range(4):
+                for g in range(2):
+                    mx(acc[:, t * P : (t + 1) * P], codes, g * BANK + t * P,
+                       quantised["x"], 256 * g + m * P, P, g == 0, g == 1)
+            return acc
+
+        def multiply_half(h, wide, narrow, m):
+            w = width_of(h)
+            acc = next_bank()
+            mx(acc[:, 0:w], quantised["x"], m * P, wide, 0, w, True, False)
+            mx(acc[:, 0:w], quantised["x"], 256 + m * P, wide, w, w, False, False)
+            mx(acc[:, 0:w], quantised[h % 2], m * P, narrow, 0, w, False, True)
+            return acc
+
+        def round_p(n, acc, m, on_vector):
+            if m == 0:
+                rounded[n] = const.tile([P, 4 * T], BF16, name="pg%d" % n, align_bytes=64)
+            copy_by(
+                on_vector,
+                rounded[n][:, m * BANK : (m + 1) * BANK].rearrange("q (n t) -> q n t", t=4),
+                acc[:].rearrange("q (t n) -> q n t", t=4),
+            )
+
+        def finish(h, acc, m):
+            w = width_of(h)
+            by_row = acc[:, 0:w].rearrange("t (j p) -> t p j", p=P)
+            if h % 2 == 0:
+                gated = act.tile([P, BANK], F32, tag="silu", name="silu")
+                nc.scalar.activation(out=gated[:, 0:w].rearrange("t (p j) -> t p j", p=P), in_=by_row, func=SILU)
                 silu_of[m] = gated
-            if kind == "half" and n % 2 == 1:
-                c = n // 2
-                z = res.tile([P, CHUNK], F32, tag="o", name="o")
+            else:
+                c = h // 2
+                z = res.tile([P, BANK], F32, tag="o", name="o")
                 nc.vector.tensor_tensor(
-                    out=as_rows(z[:]),
-                    in0=by_row(accs[m][:]),
-                    in1=as_rows(silu_of[m][:]),
+                    out=z[:, 0:w].rearrange("t (p j) -> t p j", p=P),
+                    in0=by_row,
+                    in1=silu_of[m][:, 0:w].rearrange("t (p j) -> t p j", p=P),
                     op=mybir.AluOpType.mult,
                 )
-                nc.sync.dma_start(out=out_tiles[m][:, c * CHUNK : (c + 1) * CHUNK], in_=z[:])
+                nc.sync.dma_start(out=out_tiles[m][:, STARTS[c] : STARTS[c] + w], in_=z[:, 0:w])
 
-        x_raw = load_rows("d", x, 2)
-        dv_raw = [load_rows("w", dv1, 4), load_rows("w", dv3, 4)]
+        idle = const.tile([P, BANK], BF16, name="idle")
+        nc.vector.memset(idle[:], 0.0)
+
+        def keep_warm(count):
+            bank = next_bank()
+            for i in range(count):
+                nc.tensor.matmul(bank[:], lhsT=idle[:, 0:P], rhs=idle[:], start=True, stop=True)
+
+        x_raw = load_rows("d", x)
+        dv_raw = [load_dv(dv1), load_dv(dv3)]
         for c in range(PRELOAD):
-            load_next_chunk()
+            load_chunk(c)
+        loaded = [PRELOAD]
 
-        work = [("x", 0), ("dv", 0), ("dv", 1)]
-        work.extend([("half", h) for h in range(2 * N_CHUNKS)])
-        work.append(("end", 0))
+        def load_next():
+            load_chunk(loaded[0])
+            loaded[0] += 1
 
-        before = ("start", 0)
-        operands = []
-        sorted_x[0] = sort_words(const, "x_sorted", x_raw, 8)
-        sorted_dv[0] = sort_words(srt, "sw", dv_raw[0], 8)
-        for kind, n in work:
-            banks = []
-            if kind != "end":
-                banks = transpose(kind, n)
-            if kind == "dv" and n == 1:
-                load_next_chunk()
-            accs = multiply(before[0], before[1], operands)
-            grouped = regroup(banks, copy_share(kind, n))
-            if kind == "half":
-                sort_weight(n + 1)
-            operands = quantise_operands(kind, grouped[0:2])
-            if kind == "x":
-                sorted_dv[1] = sort_words(srt, "sw", dv_raw[1], 8)
-            if kind == "dv" and n == 0:
-                sort_weight(0)
-                sort_delta(0)
-            finish(before[0], before[1], accs, 0)
-            if kind == "dv" and n == 1:
-                sort_delta(1)
-            if kind == "half" and n % 2 == 1:
-                sort_delta(n + 1)
-            operands.extend(quantise_operands(kind, grouped[2:3]))
-            if kind == "half" and n % 2 == 1:
-                sort_delta(n + 2)
-            finish(before[0], before[1], accs, 1)
-            if kind == "half" and n % 2 == 0:
-                load_next_chunk()
-            before = (kind, n)
+        def transpose_dv(n):
+            return [transpose_bank((dv_raw[n], dv_odd[n]), H // 2, (e, 2 + e), 256 * g) for g in range(2) for e in range(2)]
+
+        x_odd = take_odd(const, "x_odd", x_raw)
+        close_up(x_raw)
+        dv_odd = [take_odd(srt, "ow", dv_raw[0])]
+        close_up(dv_raw[0])
+        keep_warm(6)
+        banks = [transpose_bank((x_raw, x_odd), H // 2, (0, 1), 256 * g) for g in range(2)]
+        grouped = regroup("gd", banks, ())
+        quantised["x"] = new_codes(const, BANK, "x")
+        keep_warm(4)
+        dv_banks = transpose_dv(0)
+        quantise(quantised["x"], grouped, 0, BANK)
+        dv_odd.append(take_odd(srt, "ow", dv_raw[1]))
+        dv_grouped = regroup_dv(dv_banks, ())
+        close_up(dv_raw[1])
+        dv_codes = [new_codes(cod, 2 * BANK, "w")]
+        quantise(dv_codes[0], dv_grouped, 0, BANK)
+        quantise(dv_codes[0], dv_grouped, BANK, BANK)
+        keep_warm(3)
+        dv_banks = transpose_dv(1)
+        load_next()
+        accs = [multiply_dv(dv_codes[0], m) for m in range(2)]
+        take_odd_w(0)
+        dv_grouped = regroup_dv(dv_banks, ())
+        dv_codes.append(new_codes(cod, 2 * BANK, "w"))
+        quantise(dv_codes[1], dv_grouped, 0, BANK)
+        close_up_w(0)
+        take_odd_d(0)
+        quantise(dv_codes[1], dv_grouped, BANK, BANK)
+        close_up_d(0)
+        for m in range(2):
+            round_p(0, accs[m], m, m == 0 and False)
+        quantised[0] = new_codes(const, T, "p0")
+        wide_of = {}
+        narrow_of = {}
+        acc_of = {}
+        d_grouped = None
+        for h in range(N_HALVES + 2):
+            if h < N_HALVES:
+                w_banks, d_banks = transpose_half(h)
+            if h == 0:
+                quantise(quantised[0], rounded[0], 0, T)
+                accs = [multiply_dv(dv_codes[1], m) for m in range(2)]
+            elif h <= N_HALVES:
+                narrow_of[h - 1] = new_codes(cod, BANK, "d")
+                quantise(narrow_of[h - 1], d_grouped, 0, width_of(h - 1))
+            if h == 1:
+                round_p(1, accs[1], 1, False)
+                quantised[1] = new_codes(const, T, "p1")
+            if h >= 2:
+                finish(h - 2, acc_of[(h - 2, 1)], 1)
+            if 1 <= h <= N_HALVES:
+                for m in range(2):
+                    acc_of[(h - 1, m)] = multiply_half(h - 1, wide_of[h - 1], narrow_of[h - 1], m)
+            if h == 1:
+                quantise(quantised[1], rounded[1], 0, T)
+            if h % 2 == 1:
+                load_next()
+            if h < N_HALVES:
+                w = width_of(h)
+                w_grouped = regroup("gw", w_banks, {13: (1, 3)}.get(h, ()))
+                take_odd_w(h + 1)
+                d_grouped = regroup("gd", d_banks, {}.get(h, ()))
+                wide_of[h] = new_codes(cod, 2 * BANK, "w")
+                quantise(wide_of[h], w_grouped, 0, w)
+                close_up_w(h + 1)
+                take_odd_d(h + 1)
+                quantise(wide_of[h], w_grouped, w, w)
+                close_up_d(h + 1)
+            if h == 0:
+                round_p(1, accs[0], 0, False)
+            elif h <= N_HALVES:
+                finish(h - 1, acc_of[(h - 1, 0)], 0)

@@ -47,16 +47,23 @@ def tile_merge_mixtralsparsemoeblock_pa_kernel(
 
         def load_dv(dv):
             tile = raw.tile([P, 4 * H], BF16, tag="w", name="w")
-            nc.sync.dma_start(
-                out=tile[:].rearrange("p (h f) -> p h f", h=2),
-                in_=dv.rearrange("(h p e) k -> p h (e k)", h=2, e=2),
-            )
+            for e in range(2):
+                nc.sync.dma_start(
+                    out=tile[:, 2 * e * H : 2 * (e + 1) * H].rearrange("p (h k) -> p h k", h=2),
+                    in_=dv.rearrange("(h p e) k -> e p h k", h=2, e=2)[e],
+                )
             return tile
 
-        def load_rows(tag, src):
+        def load_rows(tag, src, parts=1):
             rows_each = src.shape[0] // P
             tile = raw.tile([P, rows_each * src.shape[1]], BF16, tag=tag, name=tag)
-            nc.sync.dma_start(out=tile[:], in_=src.rearrange("(p j) k -> p (j k)", j=rows_each))
+            n = rows_each // parts
+            k = src.shape[1]
+            for part in range(parts):
+                nc.sync.dma_start(
+                    out=tile[:, part * n * k : (part + 1) * n * k].rearrange("p (j k) -> p j k", j=n),
+                    in_=src.rearrange("(p j) k -> p j k", j=rows_each)[:, part * n : (part + 1) * n, :],
+                )
             return tile
 
         raw_w = {}
@@ -65,7 +72,7 @@ def tile_merge_mixtralsparsemoeblock_pa_kernel(
         def load_chunk(c):
             if c < N_CHUNKS:
                 rows = slice(STARTS[c], STARTS[c] + WIDTHS[c])
-                raw_w[2 * c] = load_rows("w", Wmean1[rows, :])
+                raw_w[2 * c] = load_rows("w", Wmean1[rows, :], 1 if c == 0 else 1)
                 raw_d[2 * c] = load_rows("d", du1[rows, :])
                 raw_w[2 * c + 1] = load_rows("w", Wmean3[rows, :])
                 raw_d[2 * c + 1] = load_rows("d", du3[rows, :])
@@ -83,16 +90,19 @@ def tile_merge_mixtralsparsemoeblock_pa_kernel(
             else:
                 nc.scalar.copy(out=dst, in_=src)
 
-        def take_odd(pool, tag, tile):
-            odd = pool.tile([P, tile.shape[1] // 2], BF16, tag=tag, name=tag)
-            nc.vector.tensor_copy(
-                out=odd[:].bitcast(F32).rearrange("p (b i h j) -> p b i h j", i=8, h=2, j=8),
-                in_=tile[:].bitcast(F32).rearrange("p (b h i u j) -> p b i h u j", h=2, i=8, u=2, j=8)[:, :, :, :, 1],
-            )
-            return odd
+        def new_odd(pool, tag, tile):
+            return pool.tile([P, tile.shape[1] // 2], BF16, tag=tag, name=tag)
 
-        def close_up(tile):
-            runs = tile[:].bitcast(F32).rearrange("p (b h i u j) -> p b h i u j", h=2, i=8, u=2, j=8)
+        def take_odd(odd, tile, part=0, parts=1):
+            n = tile.shape[1] // parts
+            nc.vector.tensor_copy(
+                out=odd[:, part * n // 2 : (part + 1) * n // 2].bitcast(F32).rearrange("p (b i h j) -> p b i h j", i=8, h=2, j=8),
+                in_=tile[:, part * n : (part + 1) * n].bitcast(F32).rearrange("p (b h i u j) -> p b i h u j", h=2, i=8, u=2, j=8)[:, :, :, :, 1],
+            )
+
+        def close_up(tile, part=0, parts=1):
+            n = tile.shape[1] // parts
+            runs = tile[:, part * n : (part + 1) * n].bitcast(F32).rearrange("p (b h i u j) -> p b h i u j", h=2, i=8, u=2, j=8)
             nc.vector.tensor_copy(out=runs[:, :, 0, :, 1], in_=runs[:, :, 1, :, 0])
 
         def transpose_bank(pair, row_words, groups, word0):
@@ -105,13 +115,13 @@ def tile_merge_mixtralsparsemoeblock_pa_kernel(
                     nc.tensor.transpose(bank[:, pos : pos + P], words[:, src : src + P], ident[:])
             return bank
 
-        def regroup(tag, banks, on_vector):
+        def regroup(tag, banks, on_vector, places=(0, 1, 2, 3)):
             tile = grp.tile([P, 2 * BANK * len(banks)], BF16, tag=tag, name=tag, align_bytes=64)
             words = tile[:].bitcast(F32)
             for i in range(len(banks)):
                 copy_by(
                     i in on_vector,
-                    words[:, i * BANK : (i + 1) * BANK].rearrange("q (n u) -> q n u", u=2),
+                    words[:, places[i] * BANK : (places[i] + 1) * BANK].rearrange("q (n u) -> q n u", u=2),
                     banks[i][:].rearrange("q (u n) -> q n u", u=2),
                 )
             return tile
@@ -123,7 +133,7 @@ def tile_merge_mixtralsparsemoeblock_pa_kernel(
                 for u in range(2):
                     copy_by(
                         n in on_vector,
-                        places[:, n // 2, n % 2, u].rearrange("q (i h j w) -> q i h j w", h=2, j=8, w=2),
+                        places[:, n % 2, n // 2, u].rearrange("q (i h j w) -> q i h j w", h=2, j=8, w=2),
                         banks[n][:].rearrange("q (w h i u j) -> q u i h j w", w=2, h=2, i=8, u=2)[:, u],
                     )
             return tile
@@ -165,11 +175,13 @@ def tile_merge_mixtralsparsemoeblock_pa_kernel(
 
         def take_odd_w(h):
             if h < N_HALVES:
-                odd_w[h] = take_odd(srt, "ow", raw_w[h])
+                odd_w[h] = new_odd(srt, "ow", raw_w[h])
+                take_odd(odd_w[h], raw_w[h])
 
         def take_odd_d(h):
             if h < N_HALVES:
-                odd_d[h] = take_odd(srd, "od", raw_d[h])
+                odd_d[h] = new_odd(srd, "od", raw_d[h])
+                take_odd(odd_d[h], raw_d[h])
 
         def close_up_w(h):
             if h < N_HALVES:
@@ -181,7 +193,10 @@ def tile_merge_mixtralsparsemoeblock_pa_kernel(
 
         def transpose_half(h):
             pairs = [(2 * b, 2 * b + 1) for b in range(width_of(h) // 256)]
-            w_banks = [transpose_bank((raw_w[h], odd_w[h]), H // 2, pair, 256 * g) for g in range(2) for pair in pairs]
+            if h == 0:
+                w_banks = [transpose_bank((raw_w[h], odd_w[h]), H // 2, pair, 256 * g) for pair in pairs for g in range(2)]
+            else:
+                w_banks = [transpose_bank((raw_w[h], odd_w[h]), H // 2, pair, 256 * g) for g in range(2) for pair in pairs]
             d_banks = [transpose_bank((raw_d[h], odd_d[h]), R // 2, pair, 0) for pair in pairs]
             return w_banks, d_banks
 
@@ -247,34 +262,42 @@ def tile_merge_mixtralsparsemoeblock_pa_kernel(
             loaded[0] += 1
 
         def transpose_dv(n):
-            return [transpose_bank((dv_raw[n], dv_odd[n]), H // 2, (e, 2 + e), 256 * g) for g in range(2) for e in range(2)]
+            return [transpose_bank((dv_raw[n], dv_odd[n]), H // 2, (2 * e, 2 * e + 1), 256 * g) for e in range(2) for g in range(2)]
 
-        x_odd = take_odd(const, "x_odd", x_raw)
+        def sort_dv(n, e):
+            take_odd(dv_odd[n], dv_raw[n], e, 2)
+            close_up(dv_raw[n], e, 2)
+
+        x_odd = new_odd(const, "x_odd", x_raw)
+        take_odd(x_odd, x_raw)
         close_up(x_raw)
-        dv_odd = [take_odd(srt, "ow", dv_raw[0])]
-        close_up(dv_raw[0])
-        keep_warm(6)
+        dv_odd = [new_odd(srt, "ow", dv_raw[n]) for n in range(2)]
+        sort_dv(0, 0)
+        keep_warm(8)
         banks = [transpose_bank((x_raw, x_odd), H // 2, (0, 1), 256 * g) for g in range(2)]
+        sort_dv(0, 1)
         grouped = regroup("gd", banks, ())
         quantised["x"] = new_codes(const, BANK, "x")
-        keep_warm(4)
+        keep_warm(2)
         dv_banks = transpose_dv(0)
         quantise(quantised["x"], grouped, 0, BANK)
-        dv_odd.append(take_odd(srt, "ow", dv_raw[1]))
+        sort_dv(1, 0)
         dv_grouped = regroup_dv(dv_banks, ())
-        close_up(dv_raw[1])
         dv_codes = [new_codes(cod, 2 * BANK, "w")]
+        sort_dv(1, 1)
         quantise(dv_codes[0], dv_grouped, 0, BANK)
         quantise(dv_codes[0], dv_grouped, BANK, BANK)
         keep_warm(3)
         dv_banks = transpose_dv(1)
         load_next()
         accs = [multiply_dv(dv_codes[0], m) for m in range(2)]
-        take_odd_w(0)
+        odd_w[0] = new_odd(srt, "ow", raw_w[0])
+        for part in range(1):
+            take_odd(odd_w[0], raw_w[0], part, 1)
+            close_up(raw_w[0], part, 1)
         dv_grouped = regroup_dv(dv_banks, ())
         dv_codes.append(new_codes(cod, 2 * BANK, "w"))
         quantise(dv_codes[1], dv_grouped, 0, BANK)
-        close_up_w(0)
         take_odd_d(0)
         quantise(dv_codes[1], dv_grouped, BANK, BANK)
         close_up_d(0)
@@ -308,7 +331,7 @@ def tile_merge_mixtralsparsemoeblock_pa_kernel(
                 load_next()
             if h < N_HALVES:
                 w = width_of(h)
-                w_grouped = regroup("gw", w_banks, {13: (1, 3)}.get(h, ()))
+                w_grouped = regroup("gw", w_banks, {13: (3,)}.get(h, ()), (0, 2, 1, 3) if h == 0 else (0, 1, 2, 3))
                 take_odd_w(h + 1)
                 d_grouped = regroup("gd", d_banks, {}.get(h, ()))
                 wide_of[h] = new_codes(cod, 2 * BANK, "w")

@@ -39,14 +39,14 @@ def tile_merge_mixtralsparsemoeblock_pa_kernel(
         psum = ctx.enter_context(tc.psum_pool(name="psum", bufs=1))
         ctx.enter_context(tc.manual_schedule())
 
-        ident = const.tile([P, P], F32, name="ident")
+        ident = const.tile([P, P], F32, name="ident", align_bytes=256)
         make_identity(nc, ident[:])
-        warm = const.tile([P, 8], F32, name="warm")
+        warm = const.tile([P, 8], F32, name="warm", align_bytes=256)
         nc.vector.memset(warm[:], 0.0)
         nc.scalar.activation(out=warm[:, 4:8], in_=warm[:, 0:4], func=SILU)
 
         def load_dv(dv):
-            tile = raw.tile([P, 4 * H], BF16, tag="w", name="w")
+            tile = raw.tile([P, 4 * H], BF16, tag="w", name="w", align_bytes=256)
             for e in range(2):
                 nc.sync.dma_start(
                     out=tile[:, 2 * e * H : 2 * (e + 1) * H].rearrange("p (h k) -> p h k", h=2),
@@ -56,7 +56,7 @@ def tile_merge_mixtralsparsemoeblock_pa_kernel(
 
         def load_rows(tag, src, parts=1):
             rows_each = src.shape[0] // P
-            tile = raw.tile([P, rows_each * src.shape[1]], BF16, tag=tag, name=tag)
+            tile = raw.tile([P, rows_each * src.shape[1]], BF16, tag=tag, name=tag, align_bytes=256)
             n = rows_each // parts
             k = src.shape[1]
             for part in range(parts):
@@ -91,7 +91,7 @@ def tile_merge_mixtralsparsemoeblock_pa_kernel(
                 nc.scalar.copy(out=dst, in_=src)
 
         def new_odd(pool, tag, tile):
-            return pool.tile([P, tile.shape[1] // 2], BF16, tag=tag, name=tag)
+            return pool.tile([P, tile.shape[1] // 2], BF16, tag=tag, name=tag, align_bytes=256)
 
         def take_odd(odd, tile, part=0, parts=1):
             n = tile.shape[1] // parts
@@ -116,7 +116,7 @@ def tile_merge_mixtralsparsemoeblock_pa_kernel(
             return bank
 
         def regroup(tag, banks, on_vector, places=(0, 1, 2, 3)):
-            tile = grp.tile([P, 2 * BANK * len(banks)], BF16, tag=tag, name=tag, align_bytes=64)
+            tile = grp.tile([P, 2 * BANK * len(banks)], BF16, tag=tag, name=tag, align_bytes=256)
             words = tile[:].bitcast(F32)
             for i in range(len(banks)):
                 copy_by(
@@ -127,7 +127,7 @@ def tile_merge_mixtralsparsemoeblock_pa_kernel(
             return tile
 
         def regroup_dv(banks, on_vector):
-            tile = grp.tile([P, 2 * BANK * len(banks)], BF16, tag="gw", name="gw", align_bytes=64)
+            tile = grp.tile([P, 2 * BANK * len(banks)], BF16, tag="gw", name="gw", align_bytes=256)
             places = tile[:].bitcast(F32).rearrange("q (g u e n) -> q g e u n", g=2, u=2, e=2)
             for n in range(len(banks)):
                 for u in range(2):
@@ -139,8 +139,8 @@ def tile_merge_mixtralsparsemoeblock_pa_kernel(
             return tile
 
         def new_codes(pool, width, tag):
-            codes = pool.tile([P, width], U32, tag="c" + tag, name="c" + tag, align_bytes=64)
-            scales = pool.tile([P, width], U8, tag="s" + tag, name="s" + tag, align_bytes=64)
+            codes = pool.tile([P, width], U32, tag="c" + tag, name="c" + tag, align_bytes=256)
+            scales = pool.tile([P, width], U8, tag="s" + tag, name="s" + tag, align_bytes=256)
             return (codes, scales)
 
         def quantise(pair, tile, first, width):
@@ -218,7 +218,7 @@ def tile_merge_mixtralsparsemoeblock_pa_kernel(
 
         def round_p(n, acc, m, on_vector):
             if m == 0:
-                rounded[n] = const.tile([P, 4 * T], BF16, name="pg%d" % n, align_bytes=64)
+                rounded[n] = const.tile([P, 4 * T], BF16, name="pg%d" % n, align_bytes=256)
             copy_by(
                 on_vector,
                 rounded[n][:, m * BANK : (m + 1) * BANK].rearrange("q (n t) -> q n t", t=4),
@@ -229,12 +229,12 @@ def tile_merge_mixtralsparsemoeblock_pa_kernel(
             w = width_of(h)
             by_row = acc[:, 0:w].rearrange("t (j p) -> t p j", p=P)
             if h % 2 == 0:
-                gated = act.tile([P, BANK], F32, tag="silu", name="silu")
+                gated = act.tile([P, BANK], F32, tag="silu", name="silu", align_bytes=256)
                 nc.scalar.activation(out=gated[:, 0:w].rearrange("t (p j) -> t p j", p=P), in_=by_row, func=SILU)
                 silu_of[m] = gated
             else:
                 c = h // 2
-                z = res.tile([P, BANK], F32, tag="o", name="o")
+                z = res.tile([P, BANK], F32, tag="o", name="o", align_bytes=256)
                 nc.vector.tensor_tensor(
                     out=z[:, 0:w].rearrange("t (p j) -> t p j", p=P),
                     in0=by_row,
@@ -243,7 +243,7 @@ def tile_merge_mixtralsparsemoeblock_pa_kernel(
                 )
                 nc.sync.dma_start(out=out_tiles[m][:, STARTS[c] : STARTS[c] + w], in_=z[:, 0:w])
 
-        idle = const.tile([P, BANK], BF16, name="idle")
+        idle = const.tile([P, BANK], BF16, name="idle", align_bytes=256)
         nc.vector.memset(idle[:], 0.0)
 
         def keep_warm(count):

@@ -72,7 +72,7 @@ def tile_merge_mixtralsparsemoeblock_pa_kernel(
         def load_chunk(c):
             if c < N_CHUNKS:
                 rows = slice(STARTS[c], STARTS[c] + WIDTHS[c])
-                raw_w[2 * c] = load_rows("w", Wmean1[rows, :], 1 if c == 0 else 1)
+                raw_w[2 * c] = load_rows("w", Wmean1[rows, :], 2 if c == 0 else 1)
                 raw_d[2 * c] = load_rows("d", du1[rows, :])
                 raw_w[2 * c + 1] = load_rows("w", Wmean3[rows, :])
                 raw_d[2 * c + 1] = load_rows("d", du3[rows, :])
@@ -235,13 +235,18 @@ def tile_merge_mixtralsparsemoeblock_pa_kernel(
             else:
                 c = h // 2
                 z = res.tile([P, BANK], F32, tag="o", name="o", align_bytes=256)
-                nc.vector.tensor_tensor(
-                    out=z[:, 0:w].rearrange("t (p j) -> t p j", p=P),
-                    in0=by_row,
-                    in1=silu_of[m][:, 0:w].rearrange("t (p j) -> t p j", p=P),
-                    op=mybir.AluOpType.mult,
-                )
-                nc.sync.dma_start(out=out_tiles[m][:, STARTS[c] : STARTS[c] + w], in_=z[:, 0:w])
+                pieces = 2 if h == N_HALVES - 1 and m == 1 else 1
+                n = P // pieces
+                for i in range(pieces):
+                    rows = slice(i * n, (i + 1) * n)
+                    nc.vector.tensor_tensor(
+                        out=z[:, 0:w].rearrange("t (p j) -> t p j", p=P)[:, rows],
+                        in0=by_row[:, rows],
+                        in1=silu_of[m][:, 0:w].rearrange("t (p j) -> t p j", p=P)[:, rows],
+                        op=mybir.AluOpType.mult,
+                    )
+                    cols = slice(i * w // pieces, (i + 1) * w // pieces)
+                    nc.sync.dma_start(out=out_tiles[m][:, STARTS[c] : STARTS[c] + w][:, cols], in_=z[:, cols])
 
         idle = const.tile([P, BANK], BF16, name="idle", align_bytes=256)
         nc.vector.memset(idle[:], 0.0)
@@ -292,9 +297,9 @@ def tile_merge_mixtralsparsemoeblock_pa_kernel(
         load_next()
         accs = [multiply_dv(dv_codes[0], m) for m in range(2)]
         odd_w[0] = new_odd(srt, "ow", raw_w[0])
-        for part in range(1):
-            take_odd(odd_w[0], raw_w[0], part, 1)
-            close_up(raw_w[0], part, 1)
+        for part in range(2):
+            take_odd(odd_w[0], raw_w[0], part, 2)
+            close_up(raw_w[0], part, 2)
         dv_grouped = regroup_dv(dv_banks, ())
         dv_codes.append(new_codes(cod, 2 * BANK, "w"))
         quantise(dv_codes[1], dv_grouped, 0, BANK)

@@ -313,38 +313,54 @@ def tile_merge_mixtralsparsemoeblock_pa_kernel(
         narrow_of = {}
         acc_of = {}
         d_grouped = None
+        def qd(h):
+            narrow_of[h] = new_codes(cod, BANK, "d")
+            quantise(narrow_of[h], d_of[h], 0, width_of(h))
+
+        d_of = {}
         for h in range(N_HALVES + 2):
+            steady = 1 <= h < N_HALVES
             if h < N_HALVES:
                 w_banks, d_banks = transpose_half(h)
             if h == 0:
                 quantise(quantised[0], rounded[0], 0, T)
                 accs = [multiply_dv(dv_codes[1], m) for m in range(2)]
-            elif h <= N_HALVES:
-                narrow_of[h - 1] = new_codes(cod, BANK, "d")
-                quantise(narrow_of[h - 1], d_grouped, 0, width_of(h - 1))
             if h == 1:
                 round_p(1, accs[1], 1, False)
                 quantised[1] = new_codes(const, T, "p1")
+            if steady:
+                take_odd_w(h + 1)
+            if 1 <= h <= N_HALVES:
+                qd(h - 1)
             if h >= 2:
                 finish(h - 2, acc_of[(h - 2, 1)], 1)
+            if steady:
+                close_up_w(h + 1)
+            if h == 1:
+                quantise(quantised[1], rounded[1], 0, T)
             if 1 <= h <= N_HALVES:
                 for m in range(2):
                     acc_of[(h - 1, m)] = multiply_half(h - 1, wide_of[h - 1], narrow_of[h - 1], m)
-            if h == 1:
-                quantise(quantised[1], rounded[1], 0, T)
             if h % 2 == 1:
                 load_next()
             if h < N_HALVES:
                 w = width_of(h)
                 w_grouped = regroup("gw", w_banks, {13: (3,)}.get(h, ()), (0, 2, 1, 3) if h == 0 else (0, 1, 2, 3))
-                take_odd_w(h + 1)
-                d_grouped = regroup("gd", d_banks, {}.get(h, ()))
+                if h == 0:
+                    take_odd_w(1)
+                d_of[h] = regroup("gd", d_banks, {}.get(h, ()))
                 wide_of[h] = new_codes(cod, 2 * BANK, "w")
+                if steady:
+                    take_odd_d(h + 1)
                 quantise(wide_of[h], w_grouped, 0, w)
-                close_up_w(h + 1)
-                take_odd_d(h + 1)
+                if h == 0:
+                    close_up_w(1)
+                    take_odd_d(1)
+                else:
+                    close_up_d(h + 1)
                 quantise(wide_of[h], w_grouped, w, w)
-                close_up_d(h + 1)
+                if h == 0:
+                    close_up_d(1)
             if h == 0:
                 round_p(1, accs[0], 0, False)
             elif h <= N_HALVES:

from contextlib import ExitStack

import concourse.mybir as mybir
from concourse.masks import make_identity

BF16 = mybir.dt.bfloat16
F32 = mybir.dt.float32
U32 = mybir.dt.uint32
U8 = mybir.dt.uint8
FP8X4 = mybir.dt.float8_e4m3fn_x4
SILU = mybir.ActivationFunctionType.Silu

T, H, I, R = 256, 1024, 3584, 512
P = 128
BANK = 512
N_BANKS = 8
WIDTHS = [512] * 7
STARTS = [sum(WIDTHS[:c]) for c in range(len(WIDTHS))]
N_CHUNKS = len(WIDTHS)
N_HALVES = 2 * N_CHUNKS
PRELOAD = 3

FLOPS = 2 * T * (2 * H * I + 2 * H * R + 2 * R * I)


def tile_merge_mixtralsparsemoeblock_pa_kernel(
    tc, x, Wmean1, Wmean3, du1, dv1, du3, dv3, out
):
    nc = tc.nc
    with ExitStack() as ctx:
        const = ctx.enter_context(tc.tile_pool(name="const", bufs=1))
        raw = ctx.enter_context(tc.tile_pool(name="raw", bufs=8))
        srt = ctx.enter_context(tc.tile_pool(name="srt", bufs=3))
        srd = ctx.enter_context(tc.tile_pool(name="srd", bufs=5))
        grp = ctx.enter_context(tc.tile_pool(name="grp", bufs=3))
        cod = ctx.enter_context(tc.tile_pool(name="cod", bufs=4))
        act = ctx.enter_context(tc.tile_pool(name="act", bufs=4))
        res = ctx.enter_context(tc.tile_pool(name="res", bufs=8))
        psum = ctx.enter_context(tc.psum_pool(name="psum", bufs=1))
        ctx.enter_context(tc.manual_schedule())

        ident = const.tile([P, P], F32, name="ident", align_bytes=256)
        make_identity(nc, ident[:])
        warm = const.tile([P, 8], F32, name="warm", align_bytes=256)
        nc.vector.memset(warm[:], 0.0)
        nc.scalar.activation(out=warm[:, 4:8], in_=warm[:, 0:4], func=SILU)

        def load_dv(dv):
            tile = raw.tile([P, 4 * H], BF16, tag="w", name="w", align_bytes=256)
            for e in range(2):
                nc.sync.dma_start(
                    out=tile[:, 2 * e * H : 2 * (e + 1) * H].rearrange("p (h k) -> p h k", h=2),
                    in_=dv.rearrange("(h p e) k -> e p h k", h=2, e=2)[e],
                )
            return tile

        def load_rows(tag, src, parts=1):
            rows_each = src.shape[0] // P
            tile = raw.tile([P, rows_each * src.shape[1]], BF16, tag=tag, name=tag, align_bytes=256)
            n = rows_each // parts
            k = src.shape[1]
            for part in range(parts):
                nc.sync.dma_start(
                    out=tile[:, part * n * k : (part + 1) * n * k].rearrange("p (j k) -> p j k", j=n),
                    in_=src.rearrange("(p j) k -> p j k", j=rows_each)[:, part * n : (part + 1) * n, :],
                )
            return tile

        raw_w = {}
        raw_d = {}

        def load_chunk(c):
            if c < N_CHUNKS:
                rows = slice(STARTS[c], STARTS[c] + WIDTHS[c])
                raw_w[2 * c] = load_rows("w", Wmean1[rows, :], 2 if c == 0 else 1)
                raw_d[2 * c] = load_rows("d", du1[rows, :])
                raw_w[2 * c + 1] = load_rows("w", Wmean3[rows, :])
                raw_d[2 * c + 1] = load_rows("d", du3[rows, :])

        ring = [0]

        def next_bank():
            k = ring[0] % N_BANKS
            ring[0] = ring[0] + 1
            return psum.tile([P, BANK], F32, tag="bank%d" % k, name="bank%d" % k)

        def copy_by(on_vector, dst, src):
            if on_vector:
                nc.vector.tensor_copy(out=dst, in_=src)
            else:
                nc.scalar.copy(out=dst, in_=src)

        def new_odd(pool, tag, tile):
            return pool.tile([P, tile.shape[1] // 2], BF16, tag=tag, name=tag, align_bytes=256)

        def take_odd(odd, tile, part=0, parts=1):
            n = tile.shape[1] // parts
            nc.vector.tensor_copy(
                out=odd[:, part * n // 2 : (part + 1) * n // 2].bitcast(F32).rearrange("p (b i h j) -> p b i h j", i=8, h=2, j=8),
                in_=tile[:, part * n : (part + 1) * n].bitcast(F32).rearrange("p (b h i u j) -> p b i h u j", h=2, i=8, u=2, j=8)[:, :, :, :, 1],
            )

        def close_up(tile, part=0, parts=1):
            n = tile.shape[1] // parts
            runs = tile[:, part * n : (part + 1) * n].bitcast(F32).rearrange("p (b h i u j) -> p b h i u j", h=2, i=8, u=2, j=8)
            nc.vector.tensor_copy(out=runs[:, :, 0, :, 1], in_=runs[:, :, 1, :, 0])

        def transpose_bank(pair, row_words, groups, word0):
            bank = next_bank()
            for u in range(2):
                words = pair[u][:].bitcast(F32)
                for a in range(2):
                    src = (groups[a] * row_words + word0) // (1 + u)
                    pos = (2 * u + a) * P
                    nc.tensor.transpose(bank[:, pos : pos + P], words[:, src : src + P], ident[:])
            return bank

        def regroup(tag, banks, on_vector, places=(0, 1, 2, 3)):
            tile = grp.tile([P, 2 * BANK * len(banks)], BF16, tag=tag, name=tag, align_bytes=256)
            words = tile[:].bitcast(F32)
            for i in range(len(banks)):
                copy_by(
                    i in on_vector,
                    words[:, places[i] * BANK : (places[i] + 1) * BANK].rearrange("q (n u) -> q n u", u=2),
                    banks[i][:].rearrange("q (u n) -> q n u", u=2),
                )
            return tile

        def regroup_dv(banks, on_vector):
            tile = grp.tile([P, 2 * BANK * len(banks)], BF16, tag="gw", name="gw", align_bytes=256)
            places = tile[:].bitcast(F32).rearrange("q (g u e n) -> q g e u n", g=2, u=2, e=2)
            for n in range(len(banks)):
                for u in range(2):
                    copy_by(
                        n in on_vector,
                        places[:, n % 2, n // 2, u].rearrange("q (i h j w) -> q i h j w", h=2, j=8, w=2),
                        banks[n][:].rearrange("q (w h i u j) -> q u i h j w", w=2, h=2, i=8, u=2)[:, u],
                    )
            return tile

        def new_codes(pool, width, tag):
            codes = pool.tile([P, width], U32, tag="c" + tag, name="c" + tag, align_bytes=256)
            scales = pool.tile([P, width], U8, tag="s" + tag, name="s" + tag, align_bytes=256)
            return (codes, scales)

        def quantise(pair, tile, first, width):
            columns = slice(first, first + width)
            nc.vector.quantize_mx(
                out=pair[0][:, columns].bitcast(FP8X4),
                scales=pair[1][:, columns],
                in_=tile[:, 4 * first : 4 * (first + width)],
            )

        def mx(acc, still, still0, moving, moving0, width, start, stop):
            nc.tensor.matmul_mx(
                out=acc,
                lhsT=still[0][:, still0 : still0 + P].bitcast(FP8X4),
                lhsT_scale=still[1][:, still0 : still0 + P],
                rhs=moving[0][:, moving0 : moving0 + width].bitcast(FP8X4),
                rhs_scale=moving[1][:, moving0 : moving0 + width],
                start=start,
                stop=stop,
            )

        out_tiles = out.rearrange("(p m) i -> m p i", m=2)

        quantised = {}
        rounded = {}
        odd_w = {}
        odd_d = {}
        silu_of = {}

        def width_of(h):
            return WIDTHS[h // 2]

        def take_odd_w(h):
            if h < N_HALVES:
                odd_w[h] = new_odd(srt, "ow", raw_w[h])
                take_odd(odd_w[h], raw_w[h])

        def take_odd_d(h):
            if h < N_HALVES:
                odd_d[h] = new_odd(srd, "od", raw_d[h])
                take_odd(odd_d[h], raw_d[h])

        def close_up_w(h):
            if h < N_HALVES:
                close_up(raw_w[h])

        def close_up_d(h):
            if h < N_HALVES:
                close_up(raw_d[h])

        def transpose_half(h):
            pairs = [(2 * b, 2 * b + 1) for b in range(width_of(h) // 256)]
            if h == 0:
                w_banks = [transpose_bank((raw_w[h], odd_w[h]), H // 2, pair, 256 * g) for pair in pairs for g in range(2)]
            else:
                w_banks = [transpose_bank((raw_w[h], odd_w[h]), H // 2, pair, 256 * g) for g in range(2) for pair in pairs]
            d_banks = [transpose_bank((raw_d[h], odd_d[h]), R // 2, pair, 0) for pair in pairs]
            return w_banks, d_banks

        def multiply_dv(codes, m):
            acc = next_bank()
            for t in range(4):
                for g in range(2):
                    mx(acc[:, t * P : (t + 1) * P], codes, g * BANK + t * P,
                       quantised["x"], 256 * g + m * P, P, g == 0, g == 1)
            return acc

        def multiply_half(h, wide, narrow, m):
            w = width_of(h)
            acc = next_bank()
            mx(acc[:, 0:w], quantised["x"], m * P, wide, 0, w, True, False)
            mx(acc[:, 0:w], quantised["x"], 256 + m * P, wide, w, w, False, False)
            mx(acc[:, 0:w], quantised[h % 2], m * P, narrow, 0, w, False, True)
            return acc

        def round_p(n, acc, m, on_vector):
            if m == 0:
                rounded[n] = const.tile([P, 4 * T], BF16, name="pg%d" % n, align_bytes=256)
            copy_by(
                on_vector,
                rounded[n][:, m * BANK : (m + 1) * BANK].rearrange("q (n t) -> q n t", t=4),
                acc[:].rearrange("q (t n) -> q n t", t=4),
            )

        def finish(h, acc, m):
            w = width_of(h)
            by_row = acc[:, 0:w].rearrange("t (j p) -> t p j", p=P)
            if h % 2 == 0:
                gated = act.tile([P, BANK], F32, tag="silu", name="silu", align_bytes=256)
                nc.scalar.activation(out=gated[:, 0:w].rearrange("t (p j) -> t p j", p=P), in_=by_row, func=SILU)
                silu_of[m] = gated
            else:
                c = h // 2
                z = res.tile([P, BANK], F32, tag="o", name="o", align_bytes=256)
                pieces = 2 if h == N_HALVES - 1 and m == 1 else 1
                n = P // pieces
                for i in range(pieces):
                    rows = slice(i * n, (i + 1) * n)
                    nc.vector.tensor_tensor(
                        out=z[:, 0:w].rearrange("t (p j) -> t p j", p=P)[:, rows],
                        in0=by_row[:, rows],
                        in1=silu_of[m][:, 0:w].rearrange("t (p j) -> t p j", p=P)[:, rows],
                        op=mybir.AluOpType.mult,
                    )
                    cols = slice(i * w // pieces, (i + 1) * w // pieces)
                    nc.sync.dma_start(out=out_tiles[m][:, STARTS[c] : STARTS[c] + w][:, cols], in_=z[:, cols])

        idle = const.tile([P, BANK], BF16, name="idle", align_bytes=256)
        nc.vector.memset(idle[:], 0.0)

        def keep_warm(count):
            bank = next_bank()
            for i in range(count):
                nc.tensor.matmul(bank[:], lhsT=idle[:, 0:P], rhs=idle[:], start=True, stop=True)

        x_raw = load_rows("d", x)
        dv_raw = [load_dv(dv1), load_dv(dv3)]
        for c in range(PRELOAD):
            load_chunk(c)
        loaded = [PRELOAD]

        def load_next():
            load_chunk(loaded[0])
            loaded[0] += 1

        def transpose_dv(n):
            return [transpose_bank((dv_raw[n], dv_odd[n]), H // 2, (2 * e, 2 * e + 1), 256 * g) for e in range(2) for g in range(2)]

        def sort_dv(n, e):
            take_odd(dv_odd[n], dv_raw[n], e, 2)
            close_up(dv_raw[n], e, 2)

        x_odd = new_odd(const, "x_odd", x_raw)
        take_odd(x_odd, x_raw)
        close_up(x_raw)
        dv_odd = [new_odd(srt, "ow", dv_raw[n]) for n in range(2)]
        sort_dv(0, 0)
        keep_warm(8)
        banks = [transpose_bank((x_raw, x_odd), H // 2, (0, 1), 256 * g) for g in range(2)]
        sort_dv(0, 1)
        grouped = regroup("gd", banks, ())
        quantised["x"] = new_codes(const, BANK, "x")
        keep_warm(2)
        dv_banks = transpose_dv(0)
        quantise(quantised["x"], grouped, 0, BANK)
        sort_dv(1, 0)
        dv_grouped = regroup_dv(dv_banks, ())
        dv_codes = [new_codes(cod, 2 * BANK, "w")]
        sort_dv(1, 1)
        quantise(dv_codes[0], dv_grouped, 0, BANK)
        quantise(dv_codes[0], dv_grouped, BANK, BANK)
        keep_warm(3)
        dv_banks = transpose_dv(1)
        load_next()
        accs = [multiply_dv(dv_codes[0], m) for m in range(2)]
        odd_w[0] = new_odd(srt, "ow", raw_w[0])
        for part in range(2):
            take_odd(odd_w[0], raw_w[0], part, 2)
            close_up(raw_w[0], part, 2)
        dv_grouped = regroup_dv(dv_banks, ())
        dv_codes.append(new_codes(cod, 2 * BANK, "w"))
        quantise(dv_codes[1], dv_grouped, 0, BANK)
        take_odd_d(0)
        quantise(dv_codes[1], dv_grouped, BANK, BANK)
        close_up_d(0)
        for m in range(2):
            round_p(0, accs[m], m, m == 0 and False)
        quantised[0] = new_codes(const, T, "p0")
        wide_of = {}
        narrow_of = {}
        acc_of = {}
        d_grouped = None
        def qd(h):
            narrow_of[h] = new_codes(cod, BANK, "d")
            quantise(narrow_of[h], d_of[h], 0, width_of(h))

        d_of = {}
        for h in range(N_HALVES + 2):
            steady = 1 <= h < N_HALVES
            if h < N_HALVES:
                w_banks, d_banks = transpose_half(h)
            if h == 0:
                quantise(quantised[0], rounded[0], 0, T)
                accs = [multiply_dv(dv_codes[1], m) for m in range(2)]
            if h == 1:
                round_p(1, accs[1], 1, False)
                quantised[1] = new_codes(const, T, "p1")
            if steady:
                take_odd_w(h + 1)
            if 1 <= h <= N_HALVES:
                qd(h - 1)
            if h >= 2:
                finish(h - 2, acc_of[(h - 2, 1)], 1)
            if steady:
                close_up_w(h + 1)
            if h == 1:
                quantise(quantised[1], rounded[1], 0, T)
            if 1 <= h <= N_HALVES:
                for m in range(2):
                    acc_of[(h - 1, m)] = multiply_half(h - 1, wide_of[h - 1], narrow_of[h - 1], m)
            if h % 2 == 1:
                load_next()
            if h < N_HALVES:
                w = width_of(h)
                w_grouped = regroup("gw", w_banks, {13: (3,)}.get(h, ()), (0, 2, 1, 3) if h == 0 else (0, 1, 2, 3))
                if h == 0:
                    take_odd_w(1)
                d_of[h] = regroup("gd", d_banks, {}.get(h, ()))
                wide_of[h] = new_codes(cod, 2 * BANK, "w")
                if steady:
                    take_odd_d(h + 1)
                quantise(wide_of[h], w_grouped, 0, w)
                if h == 0:
                    close_up_w(1)
                    take_odd_d(1)
                else:
                    close_up_d(h + 1)
                quantise(wide_of[h], w_grouped, w, w)
                if h == 0:
                    close_up_d(1)
            if h == 0:
                round_p(1, accs[0], 0, False)
            elif h <= N_HALVES:
                finish(h - 1, acc_of[(h - 1, 0)], 0)
